import numpy as np
import ml_dtypes


def mxq(x, axis, fmt="e4m3"):
    dtype, down = {"e4m3": (ml_dtypes.float8_e4m3fn, 7), "e5m2": (ml_dtypes.float8_e5m2, 14)}[fmt]
    v = np.moveaxis(np.asarray(x, np.float32).astype(ml_dtypes.bfloat16).astype(np.float64), axis, -1)
    blocks = v.reshape(v.shape[:-1] + (-1, 32))
    amax = np.abs(blocks).max(-1, keepdims=True)
    byte = np.maximum(np.where(amax > 0, np.frexp(amax)[1] - 1 + 127, 0) - down, 1)
    scale = np.exp2(byte - 127.0)
    codes = (blocks / scale).astype(np.float32).astype(dtype).astype(np.float64)
    return np.moveaxis((codes * scale).reshape(v.shape), -1, axis)


WIDE = False


def mx_kscale(k):
    if not WIDE:
        return np.ones(k)
    levels = np.array([20, -20, 10, -10, 0])
    a = np.random.permutation(np.resize(levels, k // 512 * 4)).reshape(k // 512, 4)
    idx = np.arange(k)
    return np.exp2(a[idx // 512, idx % 128 // 32])


BF16 = ml_dtypes.bfloat16


def bf(x):
    return np.asarray(x, np.float32).astype(BF16)


def f64(x):
    return np.asarray(x).astype(np.float64)


B, T, C, F = 4, 512, 512, 2048
M = T


def silu(v):
    return v / (1.0 + np.exp(-v))


def sigmoid(v):
    return 1.0 / (1.0 + np.exp(-v))


def setup_inputs():
    u = mx_kscale(C)
    x = bf(np.random.standard_normal((B, T, C)) + 0.5 * np.random.standard_normal((B, 1, C)))
    h = bf(silu(np.random.standard_normal((B, T, F)) * 0.85))
    memory = bf(np.random.standard_normal((1, M, C)) * 6.0 / np.sqrt(C))
    w2_0 = bf(np.random.standard_normal((F, C)) * 3.0 / np.sqrt(F))
    b2 = bf(np.random.standard_normal(C) * 0.5)
    g = bf(np.random.standard_normal((1, M, C)) * np.exp2(np.random.randint(-12, 1, (1, M, 1))) * 512.0 * u)
    gate = sigmoid(f64(h) @ f64(w2_0) + f64(b2))
    return {"h": h,
            "x": x,
            "memory": memory,
            "w2": bf(f64(w2_0) / u),
            "b2": b2,
            "gate": np.asarray(gate, np.float32),
            "grad_out": g}


def reference(h, x, memory, w2, b2, gate, grad_out):
    gt = f64(gate)
    x_mean = f64(x).mean(axis=1, keepdims=True)
    dz = f64(grad_out) * (x_mean - f64(memory)) * gt * (1.0 - gt) / B
    dh = mxq(dz.reshape(B * T, C), 1, "e5m2") @ mxq(f64(w2), 1, "e4m3").T
    return dh.reshape(B, T, F)

@@ -1,0 +1,210 @@
+from contextlib import ExitStack
+
+import concourse.mybir as mybir
+from concourse.masks import make_identity
+
+BF16 = mybir.dt.bfloat16
+F32 = mybir.dt.float32
+U32 = mybir.dt.uint32
+U8 = mybir.dt.uint8
+E4M3_X4 = mybir.dt.float8_e4m3fn_x4
+E5M2_X4 = mybir.dt.float8_e5m2_x4
+SUBTRACT = mybir.AluOpType.subtract
+MULT = mybir.AluOpType.mult
+
+P = 128
+PACK = 4
+BATCH, TOKENS, CHANNELS, HIDDEN = 4, 512, 512, 2048
+assert CHANNELS == P * PACK
+SLOT_TILES = TOKENS // P
+ROW_TILES = BATCH * SLOT_TILES
+N_TILE = 512
+F_CHUNKS = HIDDEN // N_TILE
+F_TILES = N_TILE // P
+MEAN_COLS = 32
+
+FLOPS = 2 * BATCH * TOKENS * CHANNELS * HIDDEN
+BYTES = (
+    2 * (BATCH * TOKENS * CHANNELS + 2 * TOKENS * CHANNELS + HIDDEN * CHANNELS)
+    + 4 * (BATCH * TOKENS * CHANNELS + BATCH * TOKENS * HIDDEN)
+)
+
+
+def tile_dynamicmemorybank_pb_v_kernel(tc, h, x, memory, w2, b2, gate, grad_out, out):
+    nc = tc.nc
+    with ExitStack() as ctx:
+        keep = ctx.enter_context(tc.tile_pool(name="keep", bufs=1))
+        work = ctx.enter_context(tc.tile_pool(name="work", bufs=3))
+        stage = ctx.enter_context(tc.tile_pool(name="stage", bufs=4))
+        turn_banks = ctx.enter_context(tc.psum_pool(name="turn_banks", bufs=4))
+        out_banks = ctx.enter_context(tc.psum_pool(name="out_banks", bufs=4))
+
+        w2_rows = []
+        for j in range(F_CHUNKS):
+            chunk_rows = keep.tile([P, F_TILES, CHANNELS], BF16, name="w2_rows%d" % j)
+            nc.sync.dma_start(
+                out=chunk_rows[:],
+                in_=w2[j * N_TILE : (j + 1) * N_TILE, :].rearrange("(a n) c -> n a c", n=P),
+            )
+            w2_rows.append(chunk_rows)
+
+        x_rows = [keep.tile([P, SLOT_TILES, CHANNELS], BF16, name="x_rows%d" % b) for b in range(BATCH)]
+        gate_rows = [keep.tile([P, SLOT_TILES, CHANNELS], F32, name="gate_rows%d" % b) for b in range(BATCH)]
+        mem_rows = keep.tile([P, SLOT_TILES, CHANNELS], BF16)
+        grad_rows = keep.tile([P, SLOT_TILES, CHANNELS], BF16)
+
+        def load_slots(rows, source):
+            nc.sync.dma_start(out=rows[:], in_=source.rearrange("(n a) c -> n a c", a=SLOT_TILES))
+
+        load_slots(x_rows[0], x[0, :, :])
+        load_slots(mem_rows, memory[0, :, :])
+        load_slots(grad_rows, grad_out[0, :, :])
+        load_slots(gate_rows[0], gate[0, :, :])
+        for b in range(1, BATCH):
+            load_slots(x_rows[b], x[b, :, :])
+            load_slots(gate_rows[b], gate[b, :, :])
+
+        ident_bf16 = keep.tile([P, P], BF16)
+        make_identity(nc, ident_bf16[:])
+        ident_f32 = keep.tile([P, P], F32)
+        make_identity(nc, ident_f32[:])
+        mean_weights = keep.tile([P, MEAN_COLS], BF16)
+        nc.vector.memset(mean_weights[:], 1.0 / TOKENS)
+
+        w_codes = keep.tile([P, F_CHUNKS, N_TILE], U32, align_bytes=64)
+        w_scales = keep.tile([P, F_CHUNKS, N_TILE], U8, align_bytes=64)
+        for j in range(F_CHUNKS):
+            w_grouped = work.tile([P, N_TILE, PACK], BF16, align_bytes=64)
+            for a in range(F_TILES):
+                w_turned = turn_banks.tile([P, PACK, P], BF16, tag="turn")
+                for t in range(PACK):
+                    nc.tensor.transpose(
+                        w_turned[:, t, :], w2_rows[j][:, a, t * P : (t + 1) * P], ident_bf16[:]
+                    )
+                copy_out = nc.scalar.copy if a % 2 == 0 else nc.vector.tensor_copy
+                copy_out(
+                    out=w_grouped[:, a * P : (a + 1) * P, :],
+                    in_=w_turned[:].rearrange("p t n -> p n t"),
+                )
+            nc.vector.quantize_mx(
+                out=w_codes[:, j, :].bitcast(E4M3_X4),
+                scales=w_scales[:, j, :],
+                in_=w_grouped[:].rearrange("p n t -> p (n t)"),
+            )
+
+        mem_turned = keep.tile([P, PACK, TOKENS], BF16)
+        grad4_turned = keep.tile([P, PACK, TOKENS], BF16)
+        for t in range(PACK):
+            mem_bank = turn_banks.tile([P, SLOT_TILES, P], BF16, tag="turn")
+            grad_bank = turn_banks.tile([P, SLOT_TILES, P], BF16, tag="turn")
+            for a in range(SLOT_TILES):
+                nc.tensor.transpose(mem_bank[:, a, :], mem_rows[:, a, t * P : (t + 1) * P], ident_bf16[:])
+            for a in range(SLOT_TILES):
+                nc.tensor.transpose(grad_bank[:, a, :], grad_rows[:, a, t * P : (t + 1) * P], ident_bf16[:])
+            nc.scalar.copy(out=mem_turned[:, t, :], in_=mem_bank[:].rearrange("p a n -> p (a n)"))
+            nc.scalar.mul(out=grad4_turned[:, t, :], in_=grad_bank[:].rearrange("p a n -> p (a n)"), mul=0.25)
+
+        x_mean = keep.tile([P, BATCH, PACK], F32)
+        neg_pull = [keep.tile([P, PACK, TOKENS], F32, name="neg_pull%d" % b) for b in range(BATCH)]
+
+        def pull_chunk(b, t):
+            mean_bank = turn_banks.tile([P, MEAN_COLS], F32, tag="turn")
+            for a in range(SLOT_TILES):
+                nc.tensor.matmul(
+                    out=mean_bank[:],
+                    lhsT=x_rows[b][:, a, t * P : (t + 1) * P],
+                    rhs=mean_weights[:],
+                    start=(a == 0),
+                    stop=(a == SLOT_TILES - 1),
+                )
+            nc.vector.tensor_copy(out=x_mean[:, b, t : t + 1], in_=mean_bank[:, 0:1])
+            nc.vector.scalar_tensor_tensor(
+                out=neg_pull[b][:, t, :],
+                in0=mem_turned[:, t, :],
+                scalar=x_mean[:, b, t : t + 1],
+                in1=grad4_turned[:, t, :],
+                op0=SUBTRACT,
+                op1=MULT,
+            )
+
+        for t in range(PACK):
+            pull_chunk(0, t)
+
+        neg_slopes, slope_banks, dz_groups, dz_operands = {}, {}, {}, {}
+
+        def slope(i):
+            b, a = divmod(i, SLOT_TILES)
+            neg_slope = work.tile([P, CHANNELS], F32)
+            nc.vector.scalar_tensor_tensor(
+                out=neg_slope[:],
+                in0=gate_rows[b][:, a, :],
+                scalar=1.0,
+                in1=gate_rows[b][:, a, :],
+                op0=SUBTRACT,
+                op1=MULT,
+            )
+            neg_slopes[i] = neg_slope
+
+        def turn(i):
+            slope_bank = turn_banks.tile([P, PACK, P], F32, tag="turn")
+            for t in range(PACK):
+                nc.tensor.transpose(slope_bank[:, t, :], neg_slopes[i][:, t * P : (t + 1) * P], ident_f32[:])
+            slope_banks[i] = slope_bank
+
+        def blend(i):
+            b, a = divmod(i, SLOT_TILES)
+            dz_grouped = work.tile([P, P, PACK], BF16, align_bytes=64)
+            nc.vector.tensor_tensor(
+                out=dz_grouped[:],
+                in0=slope_banks[i][:].rearrange("p t n -> p n t"),
+                in1=neg_pull[b][:, :, a * P : (a + 1) * P].rearrange("p t n -> p n t"),
+                op=MULT,
+            )
+            dz_groups[i] = dz_grouped
+
+        def quantise(i):
+            dz_codes = work.tile([P, P], U32, align_bytes=64)
+            dz_scales = work.tile([P, P], U8, align_bytes=64)
+            nc.vector.quantize_mx(
+                out=dz_codes[:].bitcast(E5M2_X4),
+                scales=dz_scales[:],
+                in_=dz_groups[i][:].rearrange("p n t -> p (n t)"),
+            )
+            dz_operands[i] = (dz_codes, dz_scales)
+
+        def multiply_and_store(i):
+            b, a = divmod(i, SLOT_TILES)
+            dz_codes, dz_scales = dz_operands[i]
+            out_rows = stage.tile([P, HIDDEN], F32)
+            for j in range(F_CHUNKS):
+                product = out_banks.tile([P, N_TILE], F32)
+                nc.tensor.matmul_mx(
+                    out=product[:],
+                    lhsT=dz_codes[:].bitcast(E5M2_X4),
+                    lhsT_scale=dz_scales[:],
+                    rhs=w_codes[:, j, :].bitcast(E4M3_X4),
+                    rhs_scale=w_scales[:, j, :],
+                    start=True,
+                    stop=True,
+                )
+                nc.scalar.copy(out=out_rows[:, j * N_TILE : (j + 1) * N_TILE], in_=product[:])
+            nc.sync.dma_start(
+                out=out[b, :, :].rearrange("(n a) f -> n a f", a=SLOT_TILES)[:, a, :], in_=out_rows[:]
+            )
+
+        def is_row_tile(i):
+            return 0 <= i < ROW_TILES
+
+        for step in range(ROW_TILES + 3):
+            if is_row_tile(step - 2):
+                blend(step - 2)
+            if is_row_tile(step):
+                slope(step)
+            if step < ROW_TILES - SLOT_TILES:
+                pull_chunk(step // SLOT_TILES + 1, step % SLOT_TILES)
+            if is_row_tile(step - 2):
+                quantise(step - 2)
+            if is_row_tile(step - 1):
+                turn(step - 1)
+            if is_row_tile(step - 3):
+                multiply_and_store(step - 3)

@@ -14,6 +14,8 @@ MULT = mybir.AluOpType.mult
 
 P = 128
 PACK = 4
+PAIR = 2
+HALVES = PACK // PAIR
 BATCH, TOKENS, CHANNELS, HIDDEN = 4, 512, 512, 2048
 assert CHANNELS == P * PACK
 SLOT_TILES = TOKENS // P
@@ -33,132 +35,143 @@ BYTES = (
 def tile_dynamicmemorybank_pb_v_kernel(tc, h, x, memory, w2, b2, gate, grad_out, out):
     nc = tc.nc
     with ExitStack() as ctx:
+        ctx.enter_context(tc.manual_schedule())
         keep = ctx.enter_context(tc.tile_pool(name="keep", bufs=1))
         work = ctx.enter_context(tc.tile_pool(name="work", bufs=3))
         stage = ctx.enter_context(tc.tile_pool(name="stage", bufs=4))
-        turn_banks = ctx.enter_context(tc.psum_pool(name="turn_banks", bufs=4))
+        turn_banks = ctx.enter_context(tc.psum_pool(name="turn_banks", bufs=2))
+        slope_pool = ctx.enter_context(tc.psum_pool(name="slope_pool", bufs=2))
         out_banks = ctx.enter_context(tc.psum_pool(name="out_banks", bufs=4))
 
-        w2_rows = []
-        for j in range(F_CHUNKS):
-            chunk_rows = keep.tile([P, F_TILES, CHANNELS], BF16, name="w2_rows%d" % j)
-            nc.sync.dma_start(
-                out=chunk_rows[:],
-                in_=w2[j * N_TILE : (j + 1) * N_TILE, :].rearrange("(a n) c -> n a c", n=P),
-            )
-            w2_rows.append(chunk_rows)
-
-        x_rows = [keep.tile([P, SLOT_TILES, CHANNELS], BF16, name="x_rows%d" % b) for b in range(BATCH)]
-        gate_rows = [keep.tile([P, SLOT_TILES, CHANNELS], F32, name="gate_rows%d" % b) for b in range(BATCH)]
-        mem_rows = keep.tile([P, SLOT_TILES, CHANNELS], BF16)
-        grad_rows = keep.tile([P, SLOT_TILES, CHANNELS], BF16)
-
-        def load_slots(rows, source):
+        def load_rows(name, dtype, source):
+            rows = keep.tile([P, SLOT_TILES, CHANNELS], dtype, name=name)
             nc.sync.dma_start(out=rows[:], in_=source.rearrange("(n a) c -> n a c", a=SLOT_TILES))
+            return rows
 
-        load_slots(x_rows[0], x[0, :, :])
-        load_slots(mem_rows, memory[0, :, :])
-        load_slots(grad_rows, grad_out[0, :, :])
-        load_slots(gate_rows[0], gate[0, :, :])
+        x_rows, gate_rows = {}, {}
+        x_rows[0] = load_rows("x_rows0", BF16, x[0, :, :])
+        mem_rows = load_rows("mem_rows", BF16, memory[0, :, :])
+        grad_rows = load_rows("grad_rows", BF16, grad_out[0, :, :])
+        w2_rows = [
+            load_rows("w2_rows%d" % j, BF16, w2[j * N_TILE : (j + 1) * N_TILE, :]) for j in range(F_CHUNKS)
+        ]
+        gate_rows[0] = keep.tile([P, SLOT_TILES, CHANNELS], F32, name="gate_rows0")
+        for a in range(SLOT_TILES):
+            nc.sync.dma_start(
+                out=gate_rows[0][:, a, :],
+                in_=gate[0, :, :].rearrange("(n a) c -> n a c", a=SLOT_TILES)[:, a, :],
+            )
         for b in range(1, BATCH):
-            load_slots(x_rows[b], x[b, :, :])
-            load_slots(gate_rows[b], gate[b, :, :])
+            x_rows[b] = load_rows("x_rows%d" % b, BF16, x[b, :, :])
+            gate_rows[b] = load_rows("gate_rows%d" % b, F32, gate[b, :, :])
 
-        ident_bf16 = keep.tile([P, P], BF16)
-        make_identity(nc, ident_bf16[:])
         ident_f32 = keep.tile([P, P], F32)
         make_identity(nc, ident_f32[:])
         mean_weights = keep.tile([P, MEAN_COLS], BF16)
         nc.vector.memset(mean_weights[:], 1.0 / TOKENS)
 
-        w_codes = keep.tile([P, F_CHUNKS, N_TILE], U32, align_bytes=64)
-        w_scales = keep.tile([P, F_CHUNKS, N_TILE], U8, align_bytes=64)
-        for j in range(F_CHUNKS):
-            w_grouped = work.tile([P, N_TILE, PACK], BF16, align_bytes=64)
-            for a in range(F_TILES):
-                w_turned = turn_banks.tile([P, PACK, P], BF16, tag="turn")
-                for t in range(PACK):
-                    nc.tensor.transpose(
-                        w_turned[:, t, :], w2_rows[j][:, a, t * P : (t + 1) * P], ident_bf16[:]
-                    )
-                copy_out = nc.scalar.copy if a % 2 == 0 else nc.vector.tensor_copy
-                copy_out(
-                    out=w_grouped[:, a * P : (a + 1) * P, :],
-                    in_=w_turned[:].rearrange("p t n -> p n t"),
-                )
-            nc.vector.quantize_mx(
-                out=w_codes[:, j, :].bitcast(E4M3_X4),
-                scales=w_scales[:, j, :],
-                in_=w_grouped[:].rearrange("p n t -> p (n t)"),
-            )
-
-        mem_turned = keep.tile([P, PACK, TOKENS], BF16)
-        grad4_turned = keep.tile([P, PACK, TOKENS], BF16)
-        for t in range(PACK):
-            mem_bank = turn_banks.tile([P, SLOT_TILES, P], BF16, tag="turn")
-            grad_bank = turn_banks.tile([P, SLOT_TILES, P], BF16, tag="turn")
-            for a in range(SLOT_TILES):
-                nc.tensor.transpose(mem_bank[:, a, :], mem_rows[:, a, t * P : (t + 1) * P], ident_bf16[:])
-            for a in range(SLOT_TILES):
-                nc.tensor.transpose(grad_bank[:, a, :], grad_rows[:, a, t * P : (t + 1) * P], ident_bf16[:])
-            nc.scalar.copy(out=mem_turned[:, t, :], in_=mem_bank[:].rearrange("p a n -> p (a n)"))
-            nc.scalar.mul(out=grad4_turned[:, t, :], in_=grad_bank[:].rearrange("p a n -> p (a n)"), mul=0.25)
+        def turn_words(bank_plane, rows, a, u):
+            nc.tensor.transpose(bank_plane, rows[:, a, :].bitcast(F32)[:, u * P : (u + 1) * P], ident_f32[:])
 
         x_mean = keep.tile([P, BATCH, PACK], F32)
+        mem_turned = keep.tile([P, HALVES * TOKENS * PAIR], BF16)
+        grad_turned = keep.tile([P, HALVES * TOKENS * PAIR], BF16)
         neg_pull = [keep.tile([P, PACK, TOKENS], F32, name="neg_pull%d" % b) for b in range(BATCH)]
 
-        def pull_chunk(b, t):
+        def turn_slots(rows, turned, copy_out):
+            for u in range(HALVES):
+                bank = turn_banks.tile([P, SLOT_TILES, P], F32, tag="turn")
+                for a in range(SLOT_TILES):
+                    turn_words(bank[:, a, :], rows, a, u)
+                copy_out(
+                    out=turned[:].bitcast(F32)[:, u * TOKENS : (u + 1) * TOKENS],
+                    in_=bank[:].rearrange("p a n -> p (a n)"),
+                )
+
+        def mean_chunk(b, k):
+            u, e = divmod(k, PAIR)
             mean_bank = turn_banks.tile([P, MEAN_COLS], F32, tag="turn")
             for a in range(SLOT_TILES):
                 nc.tensor.matmul(
                     out=mean_bank[:],
-                    lhsT=x_rows[b][:, a, t * P : (t + 1) * P],
+                    lhsT=x_rows[b][:, a, :].rearrange("n (u p e) -> n u e p", u=HALVES, e=PAIR)[:, u, e, :],
                     rhs=mean_weights[:],
                     start=(a == 0),
                     stop=(a == SLOT_TILES - 1),
                 )
-            nc.vector.tensor_copy(out=x_mean[:, b, t : t + 1], in_=mean_bank[:, 0:1])
+            nc.vector.tensor_copy(out=x_mean[:, b, k : k + 1], in_=mean_bank[:, 0:1])
+
+        def pull_chunk(b, k):
+            u, e = divmod(k, PAIR)
             nc.vector.scalar_tensor_tensor(
-                out=neg_pull[b][:, t, :],
-                in0=mem_turned[:, t, :],
-                scalar=x_mean[:, b, t : t + 1],
-                in1=grad4_turned[:, t, :],
+                out=neg_pull[b][:, k, :],
+                in0=mem_turned[:].rearrange("p (u m e) -> p u e m", u=HALVES, e=PAIR)[:, u, e, :],
+                scalar=x_mean[:, b, k : k + 1],
+                in1=grad_turned[:].rearrange("p (u m e) -> p u e m", u=HALVES, e=PAIR)[:, u, e, :],
                 op0=SUBTRACT,
                 op1=MULT,
             )
 
-        for t in range(PACK):
-            pull_chunk(0, t)
+        for k in range(PACK):
+            mean_chunk(0, k)
+        turn_slots(mem_rows, mem_turned, nc.vector.tensor_copy)
+        turn_slots(grad_rows, grad_turned, nc.scalar.copy)
+        for k in range(PACK):
+            pull_chunk(0, k)
+
+        w_codes = keep.tile([P, F_CHUNKS, N_TILE], U32, align_bytes=64)
+        w_scales = keep.tile([P, F_CHUNKS, N_TILE], U8, align_bytes=64)
+
+        def prepare_w2(j):
+            w_grouped = work.tile([P, N_TILE * PACK], BF16, align_bytes=64)
+            word_groups = w_grouped[:].bitcast(F32).rearrange("p (n w) -> p n w", w=F_TILES * HALVES)
+            for first_a in range(0, F_TILES, PAIR):
+                bank = out_banks.tile([P, PACK, P], F32, tag="product")
+                for plane in range(PACK):
+                    turn_words(bank[:, plane, :], w2_rows[j], first_a + plane // HALVES, plane % HALVES)
+                nc.scalar.copy(
+                    out=word_groups[:, :, first_a * HALVES : first_a * HALVES + PACK],
+                    in_=bank[:].rearrange("p w n -> p n w"),
+                )
+            nc.vector.quantize_mx(
+                out=w_codes[:, j, :].bitcast(E4M3_X4),
+                scales=w_scales[:, j, :],
+                in_=w_grouped[:],
+            )
 
         neg_slopes, slope_banks, dz_groups, dz_operands = {}, {}, {}, {}
 
         def slope(i):
             b, a = divmod(i, SLOT_TILES)
-            neg_slope = work.tile([P, CHANNELS], F32)
-            nc.vector.scalar_tensor_tensor(
-                out=neg_slope[:],
-                in0=gate_rows[b][:, a, :],
-                scalar=1.0,
-                in1=gate_rows[b][:, a, :],
-                op0=SUBTRACT,
-                op1=MULT,
-            )
+            neg_slope = work.tile([P, PACK, P], F32)
+            for u in range(HALVES):
+                half = gate_rows[b][:, a, u * PAIR * P : (u + 1) * PAIR * P].rearrange("n (p e) -> n e p", e=PAIR)
+                nc.vector.scalar_tensor_tensor(
+                    out=neg_slope[:, u * PAIR : (u + 1) * PAIR, :],
+                    in0=half,
+                    scalar=1.0,
+                    in1=half,
+                    op0=SUBTRACT,
+                    op1=MULT,
+                )
             neg_slopes[i] = neg_slope
 
         def turn(i):
-            slope_bank = turn_banks.tile([P, PACK, P], F32, tag="turn")
-            for t in range(PACK):
-                nc.tensor.transpose(slope_bank[:, t, :], neg_slopes[i][:, t * P : (t + 1) * P], ident_f32[:])
+            slope_bank = slope_pool.tile([P, PACK, P], F32)
+            for k in range(PACK):
+                nc.tensor.transpose(slope_bank[:, k, :], neg_slopes[i][:, k, :], ident_f32[:])
             slope_banks[i] = slope_bank
 
         def blend(i):
             b, a = divmod(i, SLOT_TILES)
             dz_grouped = work.tile([P, P, PACK], BF16, align_bytes=64)
-            nc.vector.tensor_tensor(
+            nc.vector.scalar_tensor_tensor(
                 out=dz_grouped[:],
-                in0=slope_banks[i][:].rearrange("p t n -> p n t"),
-                in1=neg_pull[b][:, :, a * P : (a + 1) * P].rearrange("p t n -> p n t"),
-                op=MULT,
+                in0=slope_banks[i][:].rearrange("p k n -> p n k"),
+                scalar=1.0 / BATCH,
+                in1=neg_pull[b][:, :, a * P : (a + 1) * P].rearrange("p k n -> p n k"),
+                op0=MULT,
+                op1=MULT,
             )
             dz_groups[i] = dz_grouped
 
@@ -168,7 +181,7 @@ def tile_dynamicmemorybank_pb_v_kernel(tc, h, x, memory, w2, b2, gate, grad_out,
             nc.vector.quantize_mx(
                 out=dz_codes[:].bitcast(E5M2_X4),
                 scales=dz_scales[:],
-                in_=dz_groups[i][:].rearrange("p n t -> p (n t)"),
+                in_=dz_groups[i][:].rearrange("p n k -> p (n k)"),
             )
             dz_operands[i] = (dz_codes, dz_scales)
 
@@ -177,7 +190,7 @@ def tile_dynamicmemorybank_pb_v_kernel(tc, h, x, memory, w2, b2, gate, grad_out,
             dz_codes, dz_scales = dz_operands[i]
             out_rows = stage.tile([P, HIDDEN], F32)
             for j in range(F_CHUNKS):
-                product = out_banks.tile([P, N_TILE], F32)
+                product = out_banks.tile([P, N_TILE], F32, tag="product")
                 nc.tensor.matmul_mx(
                     out=product[:],
                     lhsT=dz_codes[:].bitcast(E5M2_X4),
@@ -192,19 +205,28 @@ def tile_dynamicmemorybank_pb_v_kernel(tc, h, x, memory, w2, b2, gate, grad_out,
                 out=out[b, :, :].rearrange("(n a) f -> n a f", a=SLOT_TILES)[:, a, :], in_=out_rows[:]
             )
 
+        FILL_STEPS = 3
+
         def is_row_tile(i):
             return 0 <= i < ROW_TILES
 
-        for step in range(ROW_TILES + 3):
+        def pipeline_step(step):
+            if FILL_STEPS <= step < FILL_STEPS + ROW_TILES - SLOT_TILES:
+                earlier_batch, k = divmod(step - FILL_STEPS, PACK)
+                mean_chunk(earlier_batch + 1, k)
+                pull_chunk(earlier_batch + 1, k)
             if is_row_tile(step - 2):
                 blend(step - 2)
             if is_row_tile(step):
                 slope(step)
-            if step < ROW_TILES - SLOT_TILES:
-                pull_chunk(step // SLOT_TILES + 1, step % SLOT_TILES)
             if is_row_tile(step - 2):
                 quantise(step - 2)
             if is_row_tile(step - 1):
                 turn(step - 1)
             if is_row_tile(step - 3):
                 multiply_and_store(step - 3)
+
+        for j in range(F_CHUNKS):
+            prepare_w2(j)
+        for step in range(ROW_TILES + FILL_STEPS):
+            pipeline_step(step)

@@ -122,7 +122,9 @@ def tile_dynamicmemorybank_pb_v_kernel(tc, h, x, memory, w2, b2, gate, grad_out,
         w_codes = keep.tile([P, F_CHUNKS, N_TILE], U32, align_bytes=64)
         w_scales = keep.tile([P, F_CHUNKS, N_TILE], U8, align_bytes=64)
 
-        def prepare_w2(j):
+        w_groups = {}
+
+        def turn_w2(j):
             w_grouped = work.tile([P, N_TILE * PACK], BF16, align_bytes=64)
             word_groups = w_grouped[:].bitcast(F32).rearrange("p (n w) -> p n w", w=F_TILES * HALVES)
             for first_a in range(0, F_TILES, PAIR):
@@ -133,10 +135,13 @@ def tile_dynamicmemorybank_pb_v_kernel(tc, h, x, memory, w2, b2, gate, grad_out,
                     out=word_groups[:, :, first_a * HALVES : first_a * HALVES + PACK],
                     in_=bank[:].rearrange("p w n -> p n w"),
                 )
+            w_groups[j] = w_grouped
+
+        def quantise_w2(j):
             nc.vector.quantize_mx(
                 out=w_codes[:, j, :].bitcast(E4M3_X4),
                 scales=w_scales[:, j, :],
-                in_=w_grouped[:],
+                in_=w_groups[j][:],
             )
 
         neg_slopes, slope_banks, dz_groups, dz_operands = {}, {}, {}, {}
@@ -189,6 +194,7 @@ def tile_dynamicmemorybank_pb_v_kernel(tc, h, x, memory, w2, b2, gate, grad_out,
             b, a = divmod(i, SLOT_TILES)
             dz_codes, dz_scales = dz_operands[i]
             out_rows = stage.tile([P, HIDDEN], F32)
+            out_slots = out[b, :, :].rearrange("(n a) f -> n a f", a=SLOT_TILES)
             for j in range(F_CHUNKS):
                 product = out_banks.tile([P, N_TILE], F32, tag="product")
                 nc.tensor.matmul_mx(
@@ -200,21 +206,23 @@ def tile_dynamicmemorybank_pb_v_kernel(tc, h, x, memory, w2, b2, gate, grad_out,
                     start=True,
                     stop=True,
                 )
-                nc.scalar.copy(out=out_rows[:, j * N_TILE : (j + 1) * N_TILE], in_=product[:])
-            nc.sync.dma_start(
-                out=out[b, :, :].rearrange("(n a) f -> n a f", a=SLOT_TILES)[:, a, :], in_=out_rows[:]
-            )
+                copy_out = nc.vector.tensor_copy if b == BATCH - 1 and j % 2 == 1 else nc.scalar.copy
+                copy_out(out=out_rows[:, j * N_TILE : (j + 1) * N_TILE], in_=product[:])
+                if i == 0:
+                    nc.sync.dma_start(
+                        out=out_slots[:, a, j * N_TILE : (j + 1) * N_TILE],
+                        in_=out_rows[:, j * N_TILE : (j + 1) * N_TILE],
+                    )
+            if i > 0:
+                nc.sync.dma_start(out=out_slots[:, a, :], in_=out_rows[:])
 
-        FILL_STEPS = 3
+        STAGES = 4
+        SLOPE_ONLY_STEPS = 2
 
         def is_row_tile(i):
             return 0 <= i < ROW_TILES
 
         def pipeline_step(step):
-            if FILL_STEPS <= step < FILL_STEPS + ROW_TILES - SLOT_TILES:
-                earlier_batch, k = divmod(step - FILL_STEPS, PACK)
-                mean_chunk(earlier_batch + 1, k)
-                pull_chunk(earlier_batch + 1, k)
             if is_row_tile(step - 2):
                 blend(step - 2)
             if is_row_tile(step):
@@ -225,8 +233,15 @@ def tile_dynamicmemorybank_pb_v_kernel(tc, h, x, memory, w2, b2, gate, grad_out,
                 turn(step - 1)
             if is_row_tile(step - 3):
                 multiply_and_store(step - 3)
+            if is_row_tile(step - 2) and step - 2 < ROW_TILES - SLOT_TILES:
+                earlier_batch, k = divmod(step - 2, PACK)
+                mean_chunk(earlier_batch + 1, k)
+                pull_chunk(earlier_batch + 1, k)
 
         for j in range(F_CHUNKS):
-            prepare_w2(j)
-        for step in range(ROW_TILES + FILL_STEPS):
+            turn_w2(j)
+            if j >= F_CHUNKS - SLOPE_ONLY_STEPS:
+                pipeline_step(j - (F_CHUNKS - SLOPE_ONLY_STEPS))
+            quantise_w2(j)
+        for step in range(SLOPE_ONLY_STEPS, ROW_TILES + STAGES - 1):
             pipeline_step(step)

@@ -73,14 +73,14 @@ def tile_dynamicmemorybank_pb_v_kernel(tc, h, x, memory, w2, b2, gate, grad_out,
         def turn_words(bank_plane, rows, a, u):
             nc.tensor.transpose(bank_plane, rows[:, a, :].bitcast(F32)[:, u * P : (u + 1) * P], ident_f32[:])
 
-        x_mean = keep.tile([P, BATCH, PACK], F32)
+        x_means = {}
         mem_turned = keep.tile([P, HALVES * TOKENS * PAIR], BF16)
         grad_turned = keep.tile([P, HALVES * TOKENS * PAIR], BF16)
         neg_pull = [keep.tile([P, PACK, TOKENS], F32, name="neg_pull%d" % b) for b in range(BATCH)]
 
         def turn_slots(rows, turned, copy_out):
             for u in range(HALVES):
-                bank = turn_banks.tile([P, SLOT_TILES, P], F32, tag="turn")
+                bank = out_banks.tile([P, SLOT_TILES, P], F32, tag="product")
                 for a in range(SLOT_TILES):
                     turn_words(bank[:, a, :], rows, a, u)
                 copy_out(
@@ -88,25 +88,32 @@ def tile_dynamicmemorybank_pb_v_kernel(tc, h, x, memory, w2, b2, gate, grad_out,
                     in_=bank[:].rearrange("p a n -> p (a n)"),
                 )
 
+        first_means = []
+
         def mean_chunk(b, k):
             u, e = divmod(k, PAIR)
-            mean_bank = turn_banks.tile([P, MEAN_COLS], F32, tag="turn")
+            if b == 0:
+                if k == 0:
+                    first_means.append(turn_banks.tile([P, PACK, MEAN_COLS], F32, tag="turn", name="first_mean_bank"))
+                mean_bank = first_means[0][:, k, :]
+            else:
+                mean_bank = turn_banks.tile([P, MEAN_COLS], F32, tag="turn", name="mean_bank")[:]
             for a in range(SLOT_TILES):
                 nc.tensor.matmul(
-                    out=mean_bank[:],
+                    out=mean_bank,
                     lhsT=x_rows[b][:, a, :].rearrange("n (u p e) -> n u e p", u=HALVES, e=PAIR)[:, u, e, :],
                     rhs=mean_weights[:],
                     start=(a == 0),
                     stop=(a == SLOT_TILES - 1),
                 )
-            nc.vector.tensor_copy(out=x_mean[:, b, k : k + 1], in_=mean_bank[:, 0:1])
+            x_means[(b, k)] = mean_bank[:, 0:1]
 
         def pull_chunk(b, k):
             u, e = divmod(k, PAIR)
             nc.vector.scalar_tensor_tensor(
                 out=neg_pull[b][:, k, :],
                 in0=mem_turned[:].rearrange("p (u m e) -> p u e m", u=HALVES, e=PAIR)[:, u, e, :],
-                scalar=x_mean[:, b, k : k + 1],
+                scalar=x_means[(b, k)],
                 in1=grad_turned[:].rearrange("p (u m e) -> p u e m", u=HALVES, e=PAIR)[:, u, e, :],
                 op0=SUBTRACT,
                 op1=MULT,
@@ -149,22 +156,22 @@ def tile_dynamicmemorybank_pb_v_kernel(tc, h, x, memory, w2, b2, gate, grad_out,
         def slope(i):
             b, a = divmod(i, SLOT_TILES)
             neg_slope = work.tile([P, PACK, P], F32)
-            for u in range(HALVES):
-                half = gate_rows[b][:, a, u * PAIR * P : (u + 1) * PAIR * P].rearrange("n (p e) -> n e p", e=PAIR)
-                nc.vector.scalar_tensor_tensor(
-                    out=neg_slope[:, u * PAIR : (u + 1) * PAIR, :],
-                    in0=half,
-                    scalar=1.0,
-                    in1=half,
-                    op0=SUBTRACT,
-                    op1=MULT,
-                )
+            sorted_gate = gate_rows[b][:, a, :].rearrange("n (q e) -> n e q", e=PAIR)
+            nc.vector.scalar_tensor_tensor(
+                out=neg_slope[:].rearrange("n (e u) p -> n e (u p)", e=PAIR),
+                in0=sorted_gate,
+                scalar=1.0,
+                in1=sorted_gate,
+                op0=SUBTRACT,
+                op1=MULT,
+            )
             neg_slopes[i] = neg_slope
 
         def turn(i):
             slope_bank = slope_pool.tile([P, PACK, P], F32)
             for k in range(PACK):
-                nc.tensor.transpose(slope_bank[:, k, :], neg_slopes[i][:, k, :], ident_f32[:])
+                u, e = divmod(k, PAIR)
+                nc.tensor.transpose(slope_bank[:, k, :], neg_slopes[i][:, e * HALVES + u, :], ident_f32[:])
             slope_banks[i] = slope_bank
 
         def blend(i):

@@ -38,7 +38,7 @@ def tile_dynamicmemorybank_pb_v_kernel(tc, h, x, memory, w2, b2, gate, grad_out,
         ctx.enter_context(tc.manual_schedule())
         keep = ctx.enter_context(tc.tile_pool(name="keep", bufs=1))
         work = ctx.enter_context(tc.tile_pool(name="work", bufs=3))
-        stage = ctx.enter_context(tc.tile_pool(name="stage", bufs=4))
+        stage = ctx.enter_context(tc.tile_pool(name="stage", bufs=8))
         turn_banks = ctx.enter_context(tc.psum_pool(name="turn_banks", bufs=2))
         slope_pool = ctx.enter_context(tc.psum_pool(name="slope_pool", bufs=2))
         out_banks = ctx.enter_context(tc.psum_pool(name="out_banks", bufs=4))
@@ -49,21 +49,28 @@ def tile_dynamicmemorybank_pb_v_kernel(tc, h, x, memory, w2, b2, gate, grad_out,
             return rows
 
         x_rows, gate_rows = {}, {}
-        x_rows[0] = load_rows("x_rows0", BF16, x[0, :, :])
         mem_rows = load_rows("mem_rows", BF16, memory[0, :, :])
         grad_rows = load_rows("grad_rows", BF16, grad_out[0, :, :])
+        x_rows[0] = load_rows("x_rows0", BF16, x[0, :, :])
         w2_rows = [
             load_rows("w2_rows%d" % j, BF16, w2[j * N_TILE : (j + 1) * N_TILE, :]) for j in range(F_CHUNKS)
         ]
         gate_rows[0] = keep.tile([P, SLOT_TILES, CHANNELS], F32, name="gate_rows0")
-        for a in range(SLOT_TILES):
+        for first_a, end_a in ((0, 1), (1, SLOT_TILES)):
             nc.sync.dma_start(
-                out=gate_rows[0][:, a, :],
-                in_=gate[0, :, :].rearrange("(n a) c -> n a c", a=SLOT_TILES)[:, a, :],
+                out=gate_rows[0][:, first_a:end_a, :],
+                in_=gate[0, :, :].rearrange("(n a) c -> n a c", a=SLOT_TILES)[:, first_a:end_a, :],
             )
-        for b in range(1, BATCH):
-            x_rows[b] = load_rows("x_rows%d" % b, BF16, x[b, :, :])
-            gate_rows[b] = load_rows("gate_rows%d" % b, F32, gate[b, :, :])
+        x_rows[1] = load_rows("x_rows1", BF16, x[1, :, :])
+        gate_rows[1] = load_rows("gate_rows1", F32, gate[1, :, :])
+
+        def load_two(name, dtype, source):
+            rows = keep.tile([P, 2, SLOT_TILES, CHANNELS], dtype, name=name)
+            nc.sync.dma_start(out=rows[:], in_=source.rearrange("g (n a) c -> n g a c", a=SLOT_TILES))
+            return rows[:, 0, :, :], rows[:, 1, :, :]
+
+        x_rows[2], x_rows[3] = load_two("x_rows23", BF16, x[2:4, :, :])
+        gate_rows[2], gate_rows[3] = load_two("gate_rows23", F32, gate[2:4, :, :])
 
         ident_f32 = keep.tile([P, P], F32)
         make_identity(nc, ident_f32[:])
@@ -119,10 +126,10 @@ def tile_dynamicmemorybank_pb_v_kernel(tc, h, x, memory, w2, b2, gate, grad_out,
                 op1=MULT,
             )
 
-        for k in range(PACK):
-            mean_chunk(0, k)
         turn_slots(mem_rows, mem_turned, nc.vector.tensor_copy)
         turn_slots(grad_rows, grad_turned, nc.scalar.copy)
+        for k in range(PACK):
+            mean_chunk(0, k)
         for k in range(PACK):
             pull_chunk(0, k)
 
@@ -215,13 +222,7 @@ def tile_dynamicmemorybank_pb_v_kernel(tc, h, x, memory, w2, b2, gate, grad_out,
                 )
                 copy_out = nc.vector.tensor_copy if b == BATCH - 1 and j % 2 == 1 else nc.scalar.copy
                 copy_out(out=out_rows[:, j * N_TILE : (j + 1) * N_TILE], in_=product[:])
-                if i == 0:
-                    nc.sync.dma_start(
-                        out=out_slots[:, a, j * N_TILE : (j + 1) * N_TILE],
-                        in_=out_rows[:, j * N_TILE : (j + 1) * N_TILE],
-                    )
-            if i > 0:
-                nc.sync.dma_start(out=out_slots[:, a, :], in_=out_rows[:])
+            nc.sync.dma_start(out=out_slots[:, a, :], in_=out_rows[:])
 
         STAGES = 4
         SLOPE_ONLY_STEPS = 2

@@ -56,7 +56,7 @@ def tile_dynamicmemorybank_pb_v_kernel(tc, h, x, memory, w2, b2, gate, grad_out,
             load_rows("w2_rows%d" % j, BF16, w2[j * N_TILE : (j + 1) * N_TILE, :]) for j in range(F_CHUNKS)
         ]
         gate_rows[0] = keep.tile([P, SLOT_TILES, CHANNELS], F32, name="gate_rows0")
-        for first_a, end_a in ((0, 1), (1, SLOT_TILES)):
+        for first_a, end_a in ((0, 1), (1, 2), (2, SLOT_TILES)):
             nc.sync.dma_start(
                 out=gate_rows[0][:, first_a:end_a, :],
                 in_=gate[0, :, :].rearrange("(n a) c -> n a c", a=SLOT_TILES)[:, first_a:end_a, :],

@@ -24,6 +24,7 @@ N_TILE = 512
 F_CHUNKS = HIDDEN // N_TILE
 F_TILES = N_TILE // P
 MEAN_COLS = 32
+DMA_BLOCK = 256
 
 FLOPS = 2 * BATCH * TOKENS * CHANNELS * HIDDEN
 BYTES = (
@@ -44,7 +45,7 @@ def tile_dynamicmemorybank_pb_v_kernel(tc, h, x, memory, w2, b2, gate, grad_out,
         out_banks = ctx.enter_context(tc.psum_pool(name="out_banks", bufs=4))
 
         def load_rows(name, dtype, source):
-            rows = keep.tile([P, SLOT_TILES, CHANNELS], dtype, name=name)
+            rows = keep.tile([P, SLOT_TILES, CHANNELS], dtype, name=name, align_bytes=DMA_BLOCK)
             nc.sync.dma_start(out=rows[:], in_=source.rearrange("(n a) c -> n a c", a=SLOT_TILES))
             return rows
 
@@ -55,7 +56,7 @@ def tile_dynamicmemorybank_pb_v_kernel(tc, h, x, memory, w2, b2, gate, grad_out,
         w2_rows = [
             load_rows("w2_rows%d" % j, BF16, w2[j * N_TILE : (j + 1) * N_TILE, :]) for j in range(F_CHUNKS)
         ]
-        gate_rows[0] = keep.tile([P, SLOT_TILES, CHANNELS], F32, name="gate_rows0")
+        gate_rows[0] = keep.tile([P, SLOT_TILES, CHANNELS], F32, name="gate_rows0", align_bytes=DMA_BLOCK)
         for first_a, end_a in ((0, 1), (1, 2), (2, SLOT_TILES)):
             nc.sync.dma_start(
                 out=gate_rows[0][:, first_a:end_a, :],
@@ -65,7 +66,7 @@ def tile_dynamicmemorybank_pb_v_kernel(tc, h, x, memory, w2, b2, gate, grad_out,
         gate_rows[1] = load_rows("gate_rows1", F32, gate[1, :, :])
 
         def load_two(name, dtype, source):
-            rows = keep.tile([P, 2, SLOT_TILES, CHANNELS], dtype, name=name)
+            rows = keep.tile([P, 2, SLOT_TILES, CHANNELS], dtype, name=name, align_bytes=DMA_BLOCK)
             nc.sync.dma_start(out=rows[:], in_=source.rearrange("g (n a) c -> n g a c", a=SLOT_TILES))
             return rows[:, 0, :, :], rows[:, 1, :, :]
 
@@ -207,7 +208,7 @@ def tile_dynamicmemorybank_pb_v_kernel(tc, h, x, memory, w2, b2, gate, grad_out,
         def multiply_and_store(i):
             b, a = divmod(i, SLOT_TILES)
             dz_codes, dz_scales = dz_operands[i]
-            out_rows = stage.tile([P, HIDDEN], F32)
+            out_rows = stage.tile([P, HIDDEN], F32, align_bytes=DMA_BLOCK)
             out_slots = out[b, :, :].rearrange("(n a) f -> n a f", a=SLOT_TILES)
             for j in range(F_CHUNKS):
                 product = out_banks.tile([P, N_TILE], F32, tag="product")

from contextlib import ExitStack

import concourse.mybir as mybir
from concourse.masks import make_identity

BF16 = mybir.dt.bfloat16
F32 = mybir.dt.float32
U32 = mybir.dt.uint32
U8 = mybir.dt.uint8
E4M3_X4 = mybir.dt.float8_e4m3fn_x4
E5M2_X4 = mybir.dt.float8_e5m2_x4
SUBTRACT = mybir.AluOpType.subtract
MULT = mybir.AluOpType.mult

P = 128
PACK = 4
PAIR = 2
HALVES = PACK // PAIR
BATCH, TOKENS, CHANNELS, HIDDEN = 4, 512, 512, 2048
assert CHANNELS == P * PACK
SLOT_TILES = TOKENS // P
ROW_TILES = BATCH * SLOT_TILES
N_TILE = 512
F_CHUNKS = HIDDEN // N_TILE
F_TILES = N_TILE // P
MEAN_COLS = 32
DMA_BLOCK = 256

FLOPS = 2 * BATCH * TOKENS * CHANNELS * HIDDEN
BYTES = (
    2 * (BATCH * TOKENS * CHANNELS + 2 * TOKENS * CHANNELS + HIDDEN * CHANNELS)
    + 4 * (BATCH * TOKENS * CHANNELS + BATCH * TOKENS * HIDDEN)
)


def tile_dynamicmemorybank_pb_v_kernel(tc, h, x, memory, w2, b2, gate, grad_out, out):
    nc = tc.nc
    with ExitStack() as ctx:
        ctx.enter_context(tc.manual_schedule())
        keep = ctx.enter_context(tc.tile_pool(name="keep", bufs=1))
        work = ctx.enter_context(tc.tile_pool(name="work", bufs=3))
        stage = ctx.enter_context(tc.tile_pool(name="stage", bufs=8))
        turn_banks = ctx.enter_context(tc.psum_pool(name="turn_banks", bufs=2))
        slope_pool = ctx.enter_context(tc.psum_pool(name="slope_pool", bufs=2))
        out_banks = ctx.enter_context(tc.psum_pool(name="out_banks", bufs=4))

        def load_rows(name, dtype, source):
            rows = keep.tile([P, SLOT_TILES, CHANNELS], dtype, name=name, align_bytes=DMA_BLOCK)
            nc.sync.dma_start(out=rows[:], in_=source.rearrange("(n a) c -> n a c", a=SLOT_TILES))
            return rows

        x_rows, gate_rows = {}, {}
        mem_rows = load_rows("mem_rows", BF16, memory[0, :, :])
        grad_rows = load_rows("grad_rows", BF16, grad_out[0, :, :])
        x_rows[0] = load_rows("x_rows0", BF16, x[0, :, :])
        w2_rows = [
            load_rows("w2_rows%d" % j, BF16, w2[j * N_TILE : (j + 1) * N_TILE, :]) for j in range(F_CHUNKS)
        ]
        gate_rows[0] = keep.tile([P, SLOT_TILES, CHANNELS], F32, name="gate_rows0", align_bytes=DMA_BLOCK)
        for first_a, end_a in ((0, 1), (1, 2), (2, SLOT_TILES)):
            nc.sync.dma_start(
                out=gate_rows[0][:, first_a:end_a, :],
                in_=gate[0, :, :].rearrange("(n a) c -> n a c", a=SLOT_TILES)[:, first_a:end_a, :],
            )
        x_rows[1] = load_rows("x_rows1", BF16, x[1, :, :])
        gate_rows[1] = load_rows("gate_rows1", F32, gate[1, :, :])

        def load_two(name, dtype, source):
            rows = keep.tile([P, 2, SLOT_TILES, CHANNELS], dtype, name=name, align_bytes=DMA_BLOCK)
            nc.sync.dma_start(out=rows[:], in_=source.rearrange("g (n a) c -> n g a c", a=SLOT_TILES))
            return rows[:, 0, :, :], rows[:, 1, :, :]

        x_rows[2], x_rows[3] = load_two("x_rows23", BF16, x[2:4, :, :])
        gate_rows[2], gate_rows[3] = load_two("gate_rows23", F32, gate[2:4, :, :])

        ident_f32 = keep.tile([P, P], F32)
        make_identity(nc, ident_f32[:])
        mean_weights = keep.tile([P, MEAN_COLS], BF16)
        nc.vector.memset(mean_weights[:], 1.0 / TOKENS)

        def turn_words(bank_plane, rows, a, u):
            nc.tensor.transpose(bank_plane, rows[:, a, :].bitcast(F32)[:, u * P : (u + 1) * P], ident_f32[:])

        x_means = {}
        mem_turned = keep.tile([P, HALVES * TOKENS * PAIR], BF16)
        grad_turned = keep.tile([P, HALVES * TOKENS * PAIR], BF16)
        neg_pull = [keep.tile([P, PACK, TOKENS], F32, name="neg_pull%d" % b) for b in range(BATCH)]

        def turn_slots(rows, turned, copy_out):
            for u in range(HALVES):
                bank = out_banks.tile([P, SLOT_TILES, P], F32, tag="product")
                for a in range(SLOT_TILES):
                    turn_words(bank[:, a, :], rows, a, u)
                copy_out(
                    out=turned[:].bitcast(F32)[:, u * TOKENS : (u + 1) * TOKENS],
                    in_=bank[:].rearrange("p a n -> p (a n)"),
                )

        first_means = []

        def mean_chunk(b, k):
            u, e = divmod(k, PAIR)
            if b == 0:
                if k == 0:
                    first_means.append(turn_banks.tile([P, PACK, MEAN_COLS], F32, tag="turn", name="first_mean_bank"))
                mean_bank = first_means[0][:, k, :]
            else:
                mean_bank = turn_banks.tile([P, MEAN_COLS], F32, tag="turn", name="mean_bank")[:]
            for a in range(SLOT_TILES):
                nc.tensor.matmul(
                    out=mean_bank,
                    lhsT=x_rows[b][:, a, :].rearrange("n (u p e) -> n u e p", u=HALVES, e=PAIR)[:, u, e, :],
                    rhs=mean_weights[:],
                    start=(a == 0),
                    stop=(a == SLOT_TILES - 1),
                )
            x_means[(b, k)] = mean_bank[:, 0:1]

        def pull_chunk(b, k):
            u, e = divmod(k, PAIR)
            nc.vector.scalar_tensor_tensor(
                out=neg_pull[b][:, k, :],
                in0=mem_turned[:].rearrange("p (u m e) -> p u e m", u=HALVES, e=PAIR)[:, u, e, :],
                scalar=x_means[(b, k)],
                in1=grad_turned[:].rearrange("p (u m e) -> p u e m", u=HALVES, e=PAIR)[:, u, e, :],
                op0=SUBTRACT,
                op1=MULT,
            )

        turn_slots(mem_rows, mem_turned, nc.vector.tensor_copy)
        turn_slots(grad_rows, grad_turned, nc.scalar.copy)
        for k in range(PACK):
            mean_chunk(0, k)
        for k in range(PACK):
            pull_chunk(0, k)

        w_codes = keep.tile([P, F_CHUNKS, N_TILE], U32, align_bytes=64)
        w_scales = keep.tile([P, F_CHUNKS, N_TILE], U8, align_bytes=64)

        w_groups = {}

        def turn_w2(j):
            w_grouped = work.tile([P, N_TILE * PACK], BF16, align_bytes=64)
            word_groups = w_grouped[:].bitcast(F32).rearrange("p (n w) -> p n w", w=F_TILES * HALVES)
            for first_a in range(0, F_TILES, PAIR):
                bank = out_banks.tile([P, PACK, P], F32, tag="product")
                for plane in range(PACK):
                    turn_words(bank[:, plane, :], w2_rows[j], first_a + plane // HALVES, plane % HALVES)
                nc.scalar.copy(
                    out=word_groups[:, :, first_a * HALVES : first_a * HALVES + PACK],
                    in_=bank[:].rearrange("p w n -> p n w"),
                )
            w_groups[j] = w_grouped

        def quantise_w2(j):
            nc.vector.quantize_mx(
                out=w_codes[:, j, :].bitcast(E4M3_X4),
                scales=w_scales[:, j, :],
                in_=w_groups[j][:],
            )

        neg_slopes, slope_banks, dz_groups, dz_operands = {}, {}, {}, {}

        def slope(i):
            b, a = divmod(i, SLOT_TILES)
            neg_slope = work.tile([P, PACK, P], F32)
            sorted_gate = gate_rows[b][:, a, :].rearrange("n (q e) -> n e q", e=PAIR)
            nc.vector.scalar_tensor_tensor(
                out=neg_slope[:].rearrange("n (e u) p -> n e (u p)", e=PAIR),
                in0=sorted_gate,
                scalar=1.0,
                in1=sorted_gate,
                op0=SUBTRACT,
                op1=MULT,
            )
            neg_slopes[i] = neg_slope

        def turn(i):
            slope_bank = slope_pool.tile([P, PACK, P], F32)
            for k in range(PACK):
                u, e = divmod(k, PAIR)
                nc.tensor.transpose(slope_bank[:, k, :], neg_slopes[i][:, e * HALVES + u, :], ident_f32[:])
            slope_banks[i] = slope_bank

        def blend(i):
            b, a = divmod(i, SLOT_TILES)
            dz_grouped = work.tile([P, P, PACK], BF16, align_bytes=64)
            nc.vector.scalar_tensor_tensor(
                out=dz_grouped[:],
                in0=slope_banks[i][:].rearrange("p k n -> p n k"),
                scalar=1.0 / BATCH,
                in1=neg_pull[b][:, :, a * P : (a + 1) * P].rearrange("p k n -> p n k"),
                op0=MULT,
                op1=MULT,
            )
            dz_groups[i] = dz_grouped

        def quantise(i):
            dz_codes = work.tile([P, P], U32, align_bytes=64)
            dz_scales = work.tile([P, P], U8, align_bytes=64)
            nc.vector.quantize_mx(
                out=dz_codes[:].bitcast(E5M2_X4),
                scales=dz_scales[:],
                in_=dz_groups[i][:].rearrange("p n k -> p (n k)"),
            )
            dz_operands[i] = (dz_codes, dz_scales)

        def multiply_and_store(i):
            b, a = divmod(i, SLOT_TILES)
            dz_codes, dz_scales = dz_operands[i]
            out_rows = stage.tile([P, HIDDEN], F32, align_bytes=DMA_BLOCK)
            out_slots = out[b, :, :].rearrange("(n a) f -> n a f", a=SLOT_TILES)
            for j in range(F_CHUNKS):
                product = out_banks.tile([P, N_TILE], F32, tag="product")
                nc.tensor.matmul_mx(
                    out=product[:],
                    lhsT=dz_codes[:].bitcast(E5M2_X4),
                    lhsT_scale=dz_scales[:],
                    rhs=w_codes[:, j, :].bitcast(E4M3_X4),
                    rhs_scale=w_scales[:, j, :],
                    start=True,
                    stop=True,
                )
                copy_out = nc.vector.tensor_copy if b == BATCH - 1 and j % 2 == 1 else nc.scalar.copy
                copy_out(out=out_rows[:, j * N_TILE : (j + 1) * N_TILE], in_=product[:])
            nc.sync.dma_start(out=out_slots[:, a, :], in_=out_rows[:])

        STAGES = 4
        SLOPE_ONLY_STEPS = 2

        def is_row_tile(i):
            return 0 <= i < ROW_TILES

        def pipeline_step(step):
            if is_row_tile(step - 2):
                blend(step - 2)
            if is_row_tile(step):
                slope(step)
            if is_row_tile(step - 2):
                quantise(step - 2)
            if is_row_tile(step - 1):
                turn(step - 1)
            if is_row_tile(step - 3):
                multiply_and_store(step - 3)
            if is_row_tile(step - 2) and step - 2 < ROW_TILES - SLOT_TILES:
                earlier_batch, k = divmod(step - 2, PACK)
                mean_chunk(earlier_batch + 1, k)
                pull_chunk(earlier_batch + 1, k)

        for j in range(F_CHUNKS):
            turn_w2(j)
            if j >= F_CHUNKS - SLOPE_ONLY_STEPS:
                pipeline_step(j - (F_CHUNKS - SLOPE_ONLY_STEPS))
            quantise_w2(j)
        for step in range(SLOPE_ONLY_STEPS, ROW_TILES + STAGES - 1):
            pipeline_step(step)
